import numpy as np
import ml_dtypes


def mxq(x, axis, fmt="e4m3"):
    dtype, down = {"e4m3": (ml_dtypes.float8_e4m3fn, 7), "e5m2": (ml_dtypes.float8_e5m2, 14)}[fmt]
    v = np.moveaxis(np.asarray(x, np.float32).astype(ml_dtypes.bfloat16).astype(np.float64), axis, -1)
    blocks = v.reshape(v.shape[:-1] + (-1, 32))
    amax = np.abs(blocks).max(-1, keepdims=True)
    byte = np.maximum(np.where(amax > 0, np.frexp(amax)[1] - 1 + 127, 0) - down, 1)
    scale = np.exp2(byte - 127.0)
    codes = (blocks / scale).astype(np.float32).astype(dtype).astype(np.float64)
    return np.moveaxis((codes * scale).reshape(v.shape), -1, axis)


WIDE = False


def mx_kscale(k):
    if not WIDE:
        return np.ones(k)
    levels = np.array([10, -10, 5, -5, 0])
    if k % 512:
        return np.exp2(np.random.permutation(np.resize(levels, k // 32))).repeat(32)
    a = np.empty((k // 512, 16))
    for p in range(k // 512):
        a[p, :8] = np.random.permutation(np.resize(levels, 8))
        for g in range(8):
            far = levels[np.abs(levels - a[p, g]) >= 10]
            a[p, g + 8] = far[np.random.randint(len(far))]
    return np.exp2(a.ravel()).repeat(32)


BF16 = ml_dtypes.bfloat16


def bf(x):
    return np.asarray(x, np.float32).astype(BF16)


def f64(x):
    return np.asarray(x).astype(np.float64)


B, S, DIM, H, C, NOPE, ROPE, VDIM = 8, 1024, 512, 8, 128, 64, 128, 128
THETA = 10000.0
EPS = 1e-6


def rope_tables():
    freqs = 1.0 / THETA ** (np.arange(0, ROPE, 2, dtype=np.float64) / ROPE)
    ang = np.outer(np.arange(S, dtype=np.float64), freqs)
    return np.cos(ang), np.sin(ang)


def setup_inputs():
    s = mx_kscale(DIM)
    return {"x": bf(np.random.standard_normal((B, S, DIM)) * s),
            "wkv_a": bf(np.random.standard_normal((C + ROPE, DIM)) / np.sqrt(DIM) / s),
            "kv_norm_w": bf(1.0 + 0.1 * np.random.standard_normal(C))}


def reference(x, wkv_a, kv_norm_w):
    kv = mxq(f64(x), 2, "e4m3") @ mxq(f64(wkv_a), 1, "e4m3").T
    kv_lat, k_raw = kv[..., :C], kv[..., C:]
    cos, sin = rope_tables()
    x0, x1 = k_raw[..., 0::2], k_raw[..., 1::2]
    r0 = x0 * cos - x1 * sin
    r1 = x0 * sin + x1 * cos
    k_pe = np.stack([r0, r1], axis=-1).reshape(B, S, ROPE)
    rms = np.sqrt(np.mean(kv_lat * kv_lat, axis=-1, keepdims=True) + EPS)
    kv_cache = kv_lat / rms * f64(kv_norm_w)
    return kv_cache, k_pe

@@ -1,0 +1,234 @@
+import math
+from contextlib import ExitStack
+
+import concourse.mybir as mybir
+from concourse.masks import make_identity
+
+F32 = mybir.dt.float32
+BF16 = mybir.dt.bfloat16
+U32 = mybir.dt.uint32
+U8 = mybir.dt.uint8
+FP8X4 = mybir.dt.float8_e4m3fn_x4
+ALU = mybir.AluOpType
+ACT = mybir.ActivationFunctionType
+
+P = 128
+BATCH, SEQ, DIM = 8, 1024, 512
+LATENT, ROPE = 128, 128
+PAIRS = ROPE // 2
+DOUBLINGS = 6
+assert 2**DOUBLINGS == PAIRS
+THETA = 10000.0
+EPS = 1e-6
+
+WORDS = DIM // 2
+PER_PARTITION = SEQ // P
+TILES = 4
+HALVES = PER_PARTITION // TILES
+GROUPS = BATCH * HALVES
+
+ROUND = 1.5 * 2.0**23
+
+FLOPS = 2 * BATCH * SEQ * DIM * (LATENT + ROPE)
+
+
+def transpose_for_quantize(nc, psum_t, identity, rows, grouped, row_tiles):
+    row_words = rows[:].bitcast(F32)
+    grouped_words = grouped[:].bitcast(F32)
+    for pair in range(row_tiles // 2):
+        flipped = psum_t.tile([P, 2, 2, P], F32)
+        for t in range(2):
+            for u in range(2):
+                row_start = (2 * pair + t) * WORDS
+                nc.tensor.transpose(
+                    flipped[:, t, u, :], row_words[:, row_start + u : row_start + WORDS : 2], identity[:]
+                )
+        nc.scalar.copy(
+            out=grouped_words[:, 2 * pair * WORDS : 2 * (pair + 1) * WORDS].rearrange(
+                "p (t r u) -> p t r u", t=2, u=2
+            ),
+            in_=flipped[:].rearrange("p t u r -> p t r u"),
+        )
+
+
+def rotation_tables(nc, const):
+    position = const.tile([P, PER_PARTITION], F32)
+    nc.gpsimd.iota(
+        position[:],
+        pattern=[[1, PER_PARTITION]],
+        base=0,
+        channel_multiplier=PER_PARTITION,
+        allow_small_or_imprecise_dtypes=True,
+    )
+    turns = const.tile([P, 2, PER_PARTITION, PAIRS], F32)
+    nc.vector.tensor_scalar_mul(
+        out=turns[:, 0, :, 0:1], in0=position[:].unsqueeze(2), scalar1=1.0 / (2.0 * math.pi)
+    )
+    for doubling in range(DOUBLINGS):
+        width = 2**doubling
+        nc.vector.tensor_scalar_mul(
+            out=turns[:, 0, :, width : 2 * width],
+            in0=turns[:, 0, :, 0:width],
+            scalar1=THETA ** (-2.0 * width / ROPE),
+        )
+    nc.vector.tensor_scalar_add(out=turns[:, 1], in0=turns[:, 0], scalar1=0.25)
+    whole = const.tile([P, 2, PER_PARTITION, PAIRS], F32)
+    nc.vector.tensor_scalar(
+        out=whole[:], in0=turns[:], scalar1=ROUND, scalar2=ROUND, op0=ALU.add, op1=ALU.subtract
+    )
+    part = const.tile([P, 2, PER_PARTITION, PAIRS], F32)
+    nc.vector.tensor_tensor(out=part[:], in0=turns[:], in1=whole[:], op=ALU.subtract)
+    cos = const.tile([P, PER_PARTITION, PAIRS], F32)
+    signed_sin = const.tile([P, PER_PARTITION, PAIRS, 2], F32)
+    nc.scalar.activation(out=signed_sin[:, :, :, 0], in_=part[:, 0], func=ACT.Sin, scale=-2.0 * math.pi)
+    nc.scalar.activation(out=signed_sin[:, :, :, 1], in_=part[:, 0], func=ACT.Sin, scale=2.0 * math.pi)
+    nc.scalar.activation(out=cos[:], in_=part[:, 1], func=ACT.Sin, scale=2.0 * math.pi)
+    return cos, signed_sin
+
+
+def tile_simplemla_pa_t_kernel(tc, x, wkv_a, kv_norm_w, out_0, out_1):
+    nc = tc.nc
+    with ExitStack() as stack:
+        const = stack.enter_context(tc.tile_pool(name="const", bufs=1))
+        resident = stack.enter_context(tc.tile_pool(name="resident", bufs=GROUPS))
+        work = stack.enter_context(tc.tile_pool(name="work", bufs=3))
+        psum_t = stack.enter_context(tc.psum_pool(name="psum_t", bufs=4))
+        psum_kv = stack.enter_context(tc.psum_pool(name="psum_kv", bufs=2))
+        stack.enter_context(tc.manual_schedule())
+
+        w_rows = const.tile([P, 2 * DIM], BF16)
+        nc.sync.dma_start(
+            out=w_rows[:].rearrange("p (a k) -> p a k", a=2),
+            in_=wkv_a.rearrange("(a p) k -> p a k", p=P),
+        )
+        gain = const.tile([P, LATENT], BF16)
+        nc.scalar.dma_start(out=gain[:], in_=kv_norm_w.partition_broadcast(P))
+        x_rows = []
+        for g in range(GROUPS):
+            b, half = divmod(g, HALVES)
+            x_group = resident.tile([P, TILES * DIM], BF16)
+            nc.sync.dma_start(
+                out=x_group[:].rearrange("p (i k) -> p i k", i=TILES),
+                in_=x[b].rearrange("(p i) k -> p i k", i=PER_PARTITION)[
+                    :, half * TILES : (half + 1) * TILES, :
+                ],
+            )
+            x_rows.append(x_group)
+
+        identity = const.tile([P, P], F32)
+        make_identity(nc, identity[:])
+        cos, signed_sin = rotation_tables(nc, const)
+
+        w_grouped = const.tile([P, 2 * DIM], BF16, align_bytes=64)
+        transpose_for_quantize(nc, psum_t, identity, w_rows, w_grouped, 2)
+        w_codes = const.tile([P, 2 * P], U32, align_bytes=64)
+        w_scales = const.tile([P, 2 * P], U8, align_bytes=64)
+        nc.vector.quantize_mx(out=w_codes[:].bitcast(FP8X4), scales=w_scales[:], in_=w_grouped[:])
+
+        grouped_of = {}
+        codes_of = {}
+        kv_of = {}
+
+        def transpose_group(g):
+            x_grouped = work.tile([P, TILES * DIM], BF16, align_bytes=64)
+            transpose_for_quantize(nc, psum_t, identity, x_rows[g], x_grouped, TILES)
+            grouped_of[g] = x_grouped
+
+        def quantise_group(g):
+            x_codes = work.tile([P, TILES * P], U32, align_bytes=64)
+            x_scales = work.tile([P, TILES * P], U8, align_bytes=64)
+            nc.vector.quantize_mx(
+                out=x_codes[:].bitcast(FP8X4), scales=x_scales[:], in_=grouped_of[g][:]
+            )
+            codes_of[g] = (x_codes, x_scales)
+
+        def project_group(g):
+            x_codes, x_scales = codes_of[g]
+            latent = psum_kv.tile([P, TILES, LATENT], F32)
+            raw = psum_kv.tile([P, TILES, ROPE], F32)
+            for t in range(TILES):
+                tokens = slice(t * P, (t + 1) * P)
+                for result, columns in ((latent, slice(0, LATENT)), (raw, slice(LATENT, LATENT + ROPE))):
+                    nc.tensor.matmul_mx(
+                        out=result[:, t, :],
+                        lhsT=x_codes[:, tokens].bitcast(FP8X4),
+                        lhsT_scale=x_scales[:, tokens],
+                        rhs=w_codes[:, columns].bitcast(FP8X4),
+                        rhs_scale=w_scales[:, columns],
+                        start=True,
+                        stop=True,
+                    )
+            squares = work.tile([P, TILES, LATENT], F32)
+            sum_squares = work.tile([P, TILES], F32)
+            for t in range(TILES):
+                nc.scalar.activation(
+                    out=squares[:, t, :],
+                    in_=latent[:, t, :],
+                    func=ACT.Square,
+                    accum_out=sum_squares[:, t : t + 1],
+                )
+            inv_rms = work.tile([P, TILES], F32)
+            nc.scalar.activation(
+                out=inv_rms[:],
+                in_=sum_squares[:],
+                func=ACT.Abs_reciprocal_sqrt,
+                scale=1.0 / LATENT,
+                bias=EPS,
+            )
+            kv_of[g] = (latent, raw, inv_rms)
+
+        def output_rows(out, g):
+            b, half = divmod(g, HALVES)
+            return out[b].rearrange("(p i) c -> p i c", i=PER_PARTITION)[
+                :, half * TILES : (half + 1) * TILES, :
+            ]
+
+        def rotate_group(g):
+            half = g % HALVES
+            here = slice(half * TILES, (half + 1) * TILES)
+            raw_pairs = kv_of[g][1][:].rearrange("p t (j e) -> p t j e", e=2)
+            direct = work.tile([P, TILES, PAIRS, 2], F32)
+            crossed = work.tile([P, TILES, PAIRS, 2], F32)
+            nc.vector.tensor_tensor(
+                out=direct[:],
+                in0=raw_pairs,
+                in1=cos[:, here, :].unsqueeze(3).to_broadcast([P, TILES, PAIRS, 2]),
+                op=ALU.mult,
+            )
+            nc.vector.tensor_tensor(
+                out=crossed[:], in0=raw_pairs[:, :, :, ::-1], in1=signed_sin[:, here, :, :], op=ALU.mult
+            )
+            k_pe = resident.tile([P, TILES, PAIRS, 2], F32)
+            nc.gpsimd.tensor_tensor(out=k_pe[:], in0=direct[:], in1=crossed[:], op=ALU.add)
+            return k_pe
+
+        def normalise_group(g):
+            latent, raw, inv_rms = kv_of[g]
+            kv_cache = resident.tile([P, TILES, LATENT], F32)
+            for t in range(TILES):
+                nc.vector.scalar_tensor_tensor(
+                    out=kv_cache[:, t, :],
+                    in0=latent[:, t, :],
+                    scalar=inv_rms[:, t : t + 1],
+                    in1=gain[:],
+                    op0=ALU.mult,
+                    op1=ALU.mult,
+                )
+            return kv_cache
+
+        for g in range(-3, GROUPS):
+            ahead, far_ahead = g + 2, g + 3
+            if g >= 0:
+                k_pe = rotate_group(g)
+            if 0 <= ahead < GROUPS:
+                quantise_group(ahead)
+            if g >= 0:
+                kv_cache = normalise_group(g)
+                nc.sync.dma_start(out=output_rows(out_0, g), in_=kv_cache[:])
+                nc.sync.dma_start(
+                    out=output_rows(out_1, g), in_=k_pe[:].rearrange("p t j e -> p t (j e)")
+                )
+            if far_ahead < GROUPS:
+                transpose_group(far_ahead)
+            if 0 <= ahead < GROUPS:
+                project_group(ahead)

@@ -32,7 +32,7 @@ ROUND = 1.5 * 2.0**23
 FLOPS = 2 * BATCH * SEQ * DIM * (LATENT + ROPE)
 
 
-def transpose_for_quantize(nc, psum_t, identity, rows, grouped, row_tiles):
+def transpose_for_quantize(nc, psum_t, identity, rows, grouped, row_tiles, copy):
     row_words = rows[:].bitcast(F32)
     grouped_words = grouped[:].bitcast(F32)
     for pair in range(row_tiles // 2):
@@ -43,7 +43,7 @@ def transpose_for_quantize(nc, psum_t, identity, rows, grouped, row_tiles):
                 nc.tensor.transpose(
                     flipped[:, t, u, :], row_words[:, row_start + u : row_start + WORDS : 2], identity[:]
                 )
-        nc.scalar.copy(
+        copy(
             out=grouped_words[:, 2 * pair * WORDS : 2 * (pair + 1) * WORDS].rearrange(
                 "p (t r u) -> p t r u", t=2, u=2
             ),
@@ -51,7 +51,7 @@ def transpose_for_quantize(nc, psum_t, identity, rows, grouped, row_tiles):
         )
 
 
-def rotation_tables(nc, const):
+def rotation_turns(nc, const):
     position = const.tile([P, PER_PARTITION], F32)
     nc.gpsimd.iota(
         position[:],
@@ -60,30 +60,42 @@ def rotation_tables(nc, const):
         channel_multiplier=PER_PARTITION,
         allow_small_or_imprecise_dtypes=True,
     )
-    turns = const.tile([P, 2, PER_PARTITION, PAIRS], F32)
+    turn = const.tile([P, PER_PARTITION, PAIRS], F32)
     nc.vector.tensor_scalar_mul(
-        out=turns[:, 0, :, 0:1], in0=position[:].unsqueeze(2), scalar1=1.0 / (2.0 * math.pi)
+        out=turn[:, :, 0:1], in0=position[:].unsqueeze(2), scalar1=1.0 / (2.0 * math.pi)
     )
     for doubling in range(DOUBLINGS):
         width = 2**doubling
         nc.vector.tensor_scalar_mul(
-            out=turns[:, 0, :, width : 2 * width],
-            in0=turns[:, 0, :, 0:width],
+            out=turn[:, :, width : 2 * width],
+            in0=turn[:, :, 0:width],
             scalar1=THETA ** (-2.0 * width / ROPE),
         )
-    nc.vector.tensor_scalar_add(out=turns[:, 1], in0=turns[:, 0], scalar1=0.25)
-    whole = const.tile([P, 2, PER_PARTITION, PAIRS], F32)
+    return turn[:].rearrange("p (h i) j -> p h (i j)", h=HALVES)
+
+
+def rotation_phases(nc, const, turn, half):
+    phases = const.tile([P, 3, TILES * PAIRS], F32, name=f"phases_{half}")
+    minus, quarter, plus = (phases[:, n] for n in range(3))
+    whole = const.tile([P, TILES * PAIRS], F32, name=f"whole_{half}")
     nc.vector.tensor_scalar(
-        out=whole[:], in0=turns[:], scalar1=ROUND, scalar2=ROUND, op0=ALU.add, op1=ALU.subtract
+        out=whole[:], in0=turn, scalar1=ROUND, scalar2=ROUND, op0=ALU.add, op1=ALU.subtract
     )
-    part = const.tile([P, 2, PER_PARTITION, PAIRS], F32)
-    nc.vector.tensor_tensor(out=part[:], in0=turns[:], in1=whole[:], op=ALU.subtract)
-    cos = const.tile([P, PER_PARTITION, PAIRS], F32)
-    signed_sin = const.tile([P, PER_PARTITION, PAIRS, 2], F32)
-    nc.scalar.activation(out=signed_sin[:, :, :, 0], in_=part[:, 0], func=ACT.Sin, scale=-2.0 * math.pi)
-    nc.scalar.activation(out=signed_sin[:, :, :, 1], in_=part[:, 0], func=ACT.Sin, scale=2.0 * math.pi)
-    nc.scalar.activation(out=cos[:], in_=part[:, 1], func=ACT.Sin, scale=2.0 * math.pi)
-    return cos, signed_sin
+    nc.vector.tensor_tensor(out=plus, in0=turn, in1=whole[:], op=ALU.subtract)
+    nc.vector.tensor_scalar_mul(out=minus, in0=plus, scalar1=-1.0)
+    least = const.tile([P, TILES * PAIRS], F32, name=f"least_{half}")
+    nc.vector.tensor_tensor(out=least[:], in0=plus, in1=minus, op=ALU.min)
+    nc.vector.tensor_scalar_add(out=quarter, in0=least[:], scalar1=0.25)
+    return phases
+
+
+def rotation_table(nc, const, phases, half):
+    table = const.tile([P, 2, 2, TILES * PAIRS], F32, name=f"table_{half}")
+    for a in range(2):
+        nc.scalar.activation(
+            out=table[:, a], in_=phases[:, 1 - a : 3 - a], func=ACT.Sin, scale=2.0 * math.pi
+        )
+    return table
 
 
 def tile_simplemla_pa_t_kernel(tc, x, wkv_a, kv_norm_w, out_0, out_1):
@@ -105,7 +117,7 @@ def tile_simplemla_pa_t_kernel(tc, x, wkv_a, kv_norm_w, out_0, out_1):
         nc.scalar.dma_start(out=gain[:], in_=kv_norm_w.partition_broadcast(P))
         x_rows = []
         for g in range(GROUPS):
-            b, half = divmod(g, HALVES)
+            half, b = divmod(g, BATCH)
             x_group = resident.tile([P, TILES * DIM], BF16)
             nc.sync.dma_start(
                 out=x_group[:].rearrange("p (i k) -> p i k", i=TILES),
@@ -115,12 +127,14 @@ def tile_simplemla_pa_t_kernel(tc, x, wkv_a, kv_norm_w, out_0, out_1):
             )
             x_rows.append(x_group)
 
+        turn = rotation_turns(nc, const)
         identity = const.tile([P, P], F32)
         make_identity(nc, identity[:])
-        cos, signed_sin = rotation_tables(nc, const)
+        tables = [rotation_table(nc, const, rotation_phases(nc, const, turn[:, 0], 0), 0)]
 
         w_grouped = const.tile([P, 2 * DIM], BF16, align_bytes=64)
-        transpose_for_quantize(nc, psum_t, identity, w_rows, w_grouped, 2)
+        transpose_for_quantize(nc, psum_t, identity, w_rows, w_grouped, 2, nc.vector.tensor_copy)
+        phases = rotation_phases(nc, const, turn[:, 1], 1)
         w_codes = const.tile([P, 2 * P], U32, align_bytes=64)
         w_scales = const.tile([P, 2 * P], U8, align_bytes=64)
         nc.vector.quantize_mx(out=w_codes[:].bitcast(FP8X4), scales=w_scales[:], in_=w_grouped[:])
@@ -131,7 +145,8 @@ def tile_simplemla_pa_t_kernel(tc, x, wkv_a, kv_norm_w, out_0, out_1):
 
         def transpose_group(g):
             x_grouped = work.tile([P, TILES * DIM], BF16, align_bytes=64)
-            transpose_for_quantize(nc, psum_t, identity, x_rows[g], x_grouped, TILES)
+            copy = nc.vector.tensor_copy if g == 1 else nc.scalar.copy
+            transpose_for_quantize(nc, psum_t, identity, x_rows[g], x_grouped, TILES, copy)
             grouped_of[g] = x_grouped
 
         def quantise_group(g):
@@ -178,28 +193,27 @@ def tile_simplemla_pa_t_kernel(tc, x, wkv_a, kv_norm_w, out_0, out_1):
             kv_of[g] = (latent, raw, inv_rms)
 
         def output_rows(out, g):
-            b, half = divmod(g, HALVES)
+            half, b = divmod(g, BATCH)
             return out[b].rearrange("(p i) c -> p i c", i=PER_PARTITION)[
                 :, half * TILES : (half + 1) * TILES, :
             ]
 
         def rotate_group(g):
-            half = g % HALVES
-            here = slice(half * TILES, (half + 1) * TILES)
-            raw_pairs = kv_of[g][1][:].rearrange("p t (j e) -> p t j e", e=2)
-            direct = work.tile([P, TILES, PAIRS, 2], F32)
-            crossed = work.tile([P, TILES, PAIRS, 2], F32)
+            half = g // BATCH
+            products = work.tile([P, 2, TILES * PAIRS, 2], F32)
             nc.vector.tensor_tensor(
-                out=direct[:],
-                in0=raw_pairs,
-                in1=cos[:, here, :].unsqueeze(3).to_broadcast([P, TILES, PAIRS, 2]),
+                out=products[:],
+                in0=kv_of[g][1][:]
+                .rearrange("p t (j a) -> p a (t j)", a=2)
+                .unsqueeze(3)
+                .to_broadcast([P, 2, TILES * PAIRS, 2]),
+                in1=tables[half][:].rearrange("p a b ij -> p a ij b"),
                 op=ALU.mult,
             )
-            nc.vector.tensor_tensor(
-                out=crossed[:], in0=raw_pairs[:, :, :, ::-1], in1=signed_sin[:, here, :, :], op=ALU.mult
+            k_pe = resident.tile([P, TILES * PAIRS, 2], F32)
+            nc.gpsimd.tensor_tensor(
+                out=k_pe[:], in0=products[:, 0], in1=products[:, 1], op=ALU.add
             )
-            k_pe = resident.tile([P, TILES, PAIRS, 2], F32)
-            nc.gpsimd.tensor_tensor(out=k_pe[:], in0=direct[:], in1=crossed[:], op=ALU.add)
             return k_pe
 
         def normalise_group(g):
@@ -226,9 +240,15 @@ def tile_simplemla_pa_t_kernel(tc, x, wkv_a, kv_norm_w, out_0, out_1):
                 kv_cache = normalise_group(g)
                 nc.sync.dma_start(out=output_rows(out_0, g), in_=kv_cache[:])
                 nc.sync.dma_start(
-                    out=output_rows(out_1, g), in_=k_pe[:].rearrange("p t j e -> p t (j e)")
+                    out=output_rows(out_1, g), in_=k_pe[:].rearrange("p (t j) b -> p t (j b)", t=TILES)
                 )
             if far_ahead < GROUPS:
                 transpose_group(far_ahead)
+            if far_ahead == 0:
+                tables.append(rotation_table(nc, const, phases, 1))
+                preload = const.tile([P, 1], F32)
+                nc.scalar.activation(
+                    out=preload[:], in_=identity[:, 0:1], func=ACT.Abs_reciprocal_sqrt, scale=1.0, bias=1.0
+                )
             if 0 <= ahead < GROUPS:
                 project_group(ahead)

@@ -16,8 +16,6 @@ P = 128
 BATCH, SEQ, DIM = 8, 1024, 512
 LATENT, ROPE = 128, 128
 PAIRS = ROPE // 2
-DOUBLINGS = 6
-assert 2**DOUBLINGS == PAIRS
 THETA = 10000.0
 EPS = 1e-6
 
@@ -32,11 +30,17 @@ ROUND = 1.5 * 2.0**23
 FLOPS = 2 * BATCH * SEQ * DIM * (LATENT + ROPE)
 
 
-def transpose_for_quantize(nc, psum_t, identity, rows, grouped, row_tiles, copy):
+def keep_tensor_busy(nc, identity, out):
+    nc.tensor.matmul(out=out, lhsT=identity[:], rhs=identity[:], start=True, stop=True)
+
+
+def transpose_for_quantize(nc, psum_t, identity, rows, grouped, copies, busy):
     row_words = rows[:].bitcast(F32)
     grouped_words = grouped[:].bitcast(F32)
-    for pair in range(row_tiles // 2):
+    for pair, copy in enumerate(copies):
         flipped = psum_t.tile([P, 2, 2, P], F32)
+        for repeat in range(busy[pair]):
+            keep_tensor_busy(nc, identity, flipped[:, 1, 1, :])
         for t in range(2):
             for u in range(2):
                 row_start = (2 * pair + t) * WORDS
@@ -64,37 +68,45 @@ def rotation_turns(nc, const):
     nc.vector.tensor_scalar_mul(
         out=turn[:, :, 0:1], in0=position[:].unsqueeze(2), scalar1=1.0 / (2.0 * math.pi)
     )
-    for doubling in range(DOUBLINGS):
-        width = 2**doubling
-        nc.vector.tensor_scalar_mul(
-            out=turn[:, :, width : 2 * width],
-            in0=turn[:, :, 0:width],
-            scalar1=THETA ** (-2.0 * width / ROPE),
-        )
+    done = 1
+    while done < PAIRS:
+        for copy in range(1, 4):
+            nc.vector.tensor_scalar_mul(
+                out=turn[:, :, copy * done : (copy + 1) * done],
+                in0=turn[:, :, 0:done],
+                scalar1=THETA ** (-2.0 * copy * done / ROPE),
+            )
+        done *= 4
     return turn[:].rearrange("p (h i) j -> p h (i j)", h=HALVES)
 
 
-def rotation_phases(nc, const, turn, half):
-    phases = const.tile([P, 3, TILES * PAIRS], F32, name=f"phases_{half}")
-    minus, quarter, plus = (phases[:, n] for n in range(3))
-    whole = const.tile([P, TILES * PAIRS], F32, name=f"whole_{half}")
-    nc.vector.tensor_scalar(
-        out=whole[:], in0=turn, scalar1=ROUND, scalar2=ROUND, op0=ALU.add, op1=ALU.subtract
+def rotation_phases(nc, const, turn):
+    whole, rest, least = (
+        [const.tile([P, TILES * PAIRS], F32, name=f"{what}_{half}") for half in range(HALVES)]
+        for what in ("whole", "rest", "least")
     )
-    nc.vector.tensor_tensor(out=plus, in0=turn, in1=whole[:], op=ALU.subtract)
-    nc.vector.tensor_scalar_mul(out=minus, in0=plus, scalar1=-1.0)
-    least = const.tile([P, TILES * PAIRS], F32, name=f"least_{half}")
-    nc.vector.tensor_tensor(out=least[:], in0=plus, in1=minus, op=ALU.min)
-    nc.vector.tensor_scalar_add(out=quarter, in0=least[:], scalar1=0.25)
-    return phases
+    for half in range(HALVES):
+        nc.vector.tensor_scalar(
+            out=whole[half][:], in0=turn[:, half], scalar1=ROUND, scalar2=ROUND, op0=ALU.add, op1=ALU.subtract
+        )
+    for half in range(HALVES):
+        nc.vector.tensor_tensor(
+            out=rest[half][:], in0=turn[:, half], in1=whole[half][:], op=ALU.subtract
+        )
+    for half in range(HALVES):
+        nc.vector.scalar_tensor_tensor(
+            out=least[half][:], in0=rest[half][:], scalar=-1.0, in1=rest[half][:], op0=ALU.mult, op1=ALU.min
+        )
+    return list(zip(rest, least))
 
 
 def rotation_table(nc, const, phases, half):
+    rest, least = phases
+    turn = 2.0 * math.pi
     table = const.tile([P, 2, 2, TILES * PAIRS], F32, name=f"table_{half}")
-    for a in range(2):
-        nc.scalar.activation(
-            out=table[:, a], in_=phases[:, 1 - a : 3 - a], func=ACT.Sin, scale=2.0 * math.pi
-        )
+    nc.scalar.activation(out=table[:, 0, 1], in_=rest[:], func=ACT.Sin, scale=turn)
+    nc.scalar.activation(out=table[:, 1, 0], in_=rest[:], func=ACT.Sin, scale=-turn)
+    nc.scalar.activation(out=table[:, 0, 0], in_=least[:], func=ACT.Sin, scale=turn, bias=math.pi / 2.0)
     return table
 
 
@@ -130,11 +142,16 @@ def tile_simplemla_pa_t_kernel(tc, x, wkv_a, kv_norm_w, out_0, out_1):
         turn = rotation_turns(nc, const)
         identity = const.tile([P, P], F32)
         make_identity(nc, identity[:])
-        tables = [rotation_table(nc, const, rotation_phases(nc, const, turn[:, 0], 0), 0)]
+        phases = rotation_phases(nc, const, turn)
+        tables = [rotation_table(nc, const, phases[0], 0)]
 
         w_grouped = const.tile([P, 2 * DIM], BF16, align_bytes=64)
-        transpose_for_quantize(nc, psum_t, identity, w_rows, w_grouped, 2, nc.vector.tensor_copy)
-        phases = rotation_phases(nc, const, turn[:, 1], 1)
+        transpose_for_quantize(nc, psum_t, identity, w_rows, w_grouped, [nc.scalar.copy], [4])
+        tables.append(rotation_table(nc, const, phases[1], 1))
+        preload = const.tile([P, 1], F32)
+        nc.scalar.activation(
+            out=preload[:], in_=identity[:, 0:1], func=ACT.Abs_reciprocal_sqrt, scale=1.0, bias=1.0
+        )
         w_codes = const.tile([P, 2 * P], U32, align_bytes=64)
         w_scales = const.tile([P, 2 * P], U8, align_bytes=64)
         nc.vector.quantize_mx(out=w_codes[:].bitcast(FP8X4), scales=w_scales[:], in_=w_grouped[:])
@@ -145,8 +162,10 @@ def tile_simplemla_pa_t_kernel(tc, x, wkv_a, kv_norm_w, out_0, out_1):
 
         def transpose_group(g):
             x_grouped = work.tile([P, TILES * DIM], BF16, align_bytes=64)
-            copy = nc.vector.tensor_copy if g == 1 else nc.scalar.copy
-            transpose_for_quantize(nc, psum_t, identity, x_rows[g], x_grouped, TILES, copy)
+            copies = {0: 2 * [nc.vector.tensor_copy], 1: [nc.vector.tensor_copy, nc.scalar.copy]}
+            transpose_for_quantize(
+                nc, psum_t, identity, x_rows[g], x_grouped, copies.get(g, 2 * [nc.scalar.copy]), (2, 1) if g < 3 else (0, 1)
+            )
             grouped_of[g] = x_grouped
 
         def quantise_group(g):
@@ -236,6 +255,9 @@ def tile_simplemla_pa_t_kernel(tc, x, wkv_a, kv_norm_w, out_0, out_1):
                 k_pe = rotate_group(g)
             if 0 <= ahead < GROUPS:
                 quantise_group(ahead)
+            if far_ahead in (2, 4):
+                table = tables[0 if far_ahead == 2 else 1]
+                nc.vector.tensor_copy(out=table[:, 1, 1], in_=table[:, 0, 0])
             if g >= 0:
                 kv_cache = normalise_group(g)
                 nc.sync.dma_start(out=output_rows(out_0, g), in_=kv_cache[:])
@@ -244,11 +266,5 @@ def tile_simplemla_pa_t_kernel(tc, x, wkv_a, kv_norm_w, out_0, out_1):
                 )
             if far_ahead < GROUPS:
                 transpose_group(far_ahead)
-            if far_ahead == 0:
-                tables.append(rotation_table(nc, const, phases, 1))
-                preload = const.tile([P, 1], F32)
-                nc.scalar.activation(
-                    out=preload[:], in_=identity[:, 0:1], func=ACT.Abs_reciprocal_sqrt, scale=1.0, bias=1.0
-                )
             if 0 <= ahead < GROUPS:
                 project_group(ahead)

@@ -34,12 +34,12 @@ def keep_tensor_busy(nc, identity, out):
     nc.tensor.matmul(out=out, lhsT=identity[:], rhs=identity[:], start=True, stop=True)
 
 
-def transpose_for_quantize(nc, psum_t, identity, rows, grouped, copies, busy):
+def transpose_words(nc, psum_t, identity, rows, busy):
     row_words = rows[:].bitcast(F32)
-    grouped_words = grouped[:].bitcast(F32)
-    for pair, copy in enumerate(copies):
+    banks = []
+    for pair, repeats in enumerate(busy):
         flipped = psum_t.tile([P, 2, 2, P], F32)
-        for repeat in range(busy[pair]):
+        for repeat in range(repeats):
             keep_tensor_busy(nc, identity, flipped[:, 1, 1, :])
         for t in range(2):
             for u in range(2):
@@ -47,6 +47,13 @@ def transpose_for_quantize(nc, psum_t, identity, rows, grouped, copies, busy):
                 nc.tensor.transpose(
                     flipped[:, t, u, :], row_words[:, row_start + u : row_start + WORDS : 2], identity[:]
                 )
+        banks.append(flipped)
+    return banks
+
+
+def group_words(banks, grouped, copies):
+    grouped_words = grouped[:].bitcast(F32)
+    for pair, (flipped, copy) in enumerate(zip(banks, copies)):
         copy(
             out=grouped_words[:, 2 * pair * WORDS : 2 * (pair + 1) * WORDS].rearrange(
                 "p (t r u) -> p t r u", t=2, u=2
@@ -125,8 +132,12 @@ def tile_simplemla_pa_t_kernel(tc, x, wkv_a, kv_norm_w, out_0, out_1):
             out=w_rows[:].rearrange("p (a k) -> p a k", a=2),
             in_=wkv_a.rearrange("(a p) k -> p a k", p=P),
         )
-        gain = const.tile([P, LATENT], BF16)
-        nc.scalar.dma_start(out=gain[:], in_=kv_norm_w.partition_broadcast(P))
+        gain_row = const.tile([P, LATENT], BF16)
+        nc.vector.memset(gain_row[:], 0.0)
+        nc.sync.dma_start(out=gain_row[0:1, :], in_=kv_norm_w.unsqueeze(0))
+        ones = const.tile([P, P], BF16)
+        nc.vector.memset(ones[:], 1.0)
+        gain = const.tile([P, LATENT], F32)
         x_rows = []
         for g in range(GROUPS):
             half, b = divmod(g, BATCH)
@@ -146,7 +157,7 @@ def tile_simplemla_pa_t_kernel(tc, x, wkv_a, kv_norm_w, out_0, out_1):
         tables = [rotation_table(nc, const, phases[0], 0)]
 
         w_grouped = const.tile([P, 2 * DIM], BF16, align_bytes=64)
-        transpose_for_quantize(nc, psum_t, identity, w_rows, w_grouped, [nc.scalar.copy], [4])
+        group_words(transpose_words(nc, psum_t, identity, w_rows, [4]), w_grouped, [nc.scalar.copy])
         tables.append(rotation_table(nc, const, phases[1], 1))
         preload = const.tile([P, 1], F32)
         nc.scalar.activation(
@@ -156,16 +167,25 @@ def tile_simplemla_pa_t_kernel(tc, x, wkv_a, kv_norm_w, out_0, out_1):
         w_scales = const.tile([P, 2 * P], U8, align_bytes=64)
         nc.vector.quantize_mx(out=w_codes[:].bitcast(FP8X4), scales=w_scales[:], in_=w_grouped[:])
 
+        banks_of = {}
         grouped_of = {}
         codes_of = {}
         kv_of = {}
+        inv_rms_of = {}
+        products_of = {}
+
+        def spread_gain():
+            spread = psum_kv.tile([P, LATENT], F32, name="raw")
+            nc.tensor.matmul(out=spread[:], lhsT=ones[:], rhs=gain_row[:], start=True, stop=True)
+            nc.vector.tensor_copy(out=gain[:], in_=spread[:])
 
         def transpose_group(g):
+            banks_of[g] = transpose_words(nc, psum_t, identity, x_rows[g], (2, 1) if g < 3 else (0, 1))
+
+        def copy_group(g):
             x_grouped = work.tile([P, TILES * DIM], BF16, align_bytes=64)
             copies = {0: 2 * [nc.vector.tensor_copy], 1: [nc.vector.tensor_copy, nc.scalar.copy]}
-            transpose_for_quantize(
-                nc, psum_t, identity, x_rows[g], x_grouped, copies.get(g, 2 * [nc.scalar.copy]), (2, 1) if g < 3 else (0, 1)
-            )
+            group_words(banks_of[g], x_grouped, copies.get(g, 2 * [nc.scalar.copy]))
             grouped_of[g] = x_grouped
 
         def quantise_group(g):
@@ -192,6 +212,10 @@ def tile_simplemla_pa_t_kernel(tc, x, wkv_a, kv_norm_w, out_0, out_1):
                         start=True,
                         stop=True,
                     )
+            kv_of[g] = (latent, raw)
+
+        def measure_group(g):
+            latent = kv_of[g][0]
             squares = work.tile([P, TILES, LATENT], F32)
             sum_squares = work.tile([P, TILES], F32)
             for t in range(TILES):
@@ -209,7 +233,7 @@ def tile_simplemla_pa_t_kernel(tc, x, wkv_a, kv_norm_w, out_0, out_1):
                 scale=1.0 / LATENT,
                 bias=EPS,
             )
-            kv_of[g] = (latent, raw, inv_rms)
+            inv_rms_of[g] = inv_rms
 
         def output_rows(out, g):
             half, b = divmod(g, BATCH)
@@ -229,14 +253,24 @@ def tile_simplemla_pa_t_kernel(tc, x, wkv_a, kv_norm_w, out_0, out_1):
                 in1=tables[half][:].rearrange("p a b ij -> p a ij b"),
                 op=ALU.mult,
             )
+            products_of[g] = products
+
+        def add_products(g, after_codes):
+            if after_codes is not None:
+                waited = work.tile([P, 1], U32)
+                nc.gpsimd.tensor_copy(out=waited[:], in_=after_codes[:, 0:1])
+            products = products_of[g]
             k_pe = resident.tile([P, TILES * PAIRS, 2], F32)
             nc.gpsimd.tensor_tensor(
                 out=k_pe[:], in0=products[:, 0], in1=products[:, 1], op=ALU.add
             )
-            return k_pe
+            nc.sync.dma_start(
+                out=output_rows(out_1, g), in_=k_pe[:].rearrange("p (t j) b -> p t (j b)", t=TILES)
+            )
 
         def normalise_group(g):
-            latent, raw, inv_rms = kv_of[g]
+            latent = kv_of[g][0]
+            inv_rms = inv_rms_of[g]
             kv_cache = resident.tile([P, TILES, LATENT], F32)
             for t in range(TILES):
                 nc.vector.scalar_tensor_tensor(
@@ -249,22 +283,26 @@ def tile_simplemla_pa_t_kernel(tc, x, wkv_a, kv_norm_w, out_0, out_1):
                 )
             return kv_cache
 
-        for g in range(-3, GROUPS):
-            ahead, far_ahead = g + 2, g + 3
-            if g >= 0:
-                k_pe = rotate_group(g)
-            if 0 <= ahead < GROUPS:
-                quantise_group(ahead)
-            if far_ahead in (2, 4):
-                table = tables[0 if far_ahead == 2 else 1]
+        for g in range(-4, GROUPS):
+            if 0 <= g + 2 < GROUPS:
+                quantise_group(g + 2)
+            if g in (-1, 1):
+                table = tables[0 if g == -1 else 1]
                 nc.vector.tensor_copy(out=table[:, 1, 1], in_=table[:, 0, 0])
+            if g >= 1:
+                add_products(g - 1, codes_of[g + 2][0] if g + 2 < GROUPS else None)
             if g >= 0:
+                rotate_group(g)
                 kv_cache = normalise_group(g)
                 nc.sync.dma_start(out=output_rows(out_0, g), in_=kv_cache[:])
-                nc.sync.dma_start(
-                    out=output_rows(out_1, g), in_=k_pe[:].rearrange("p (t j) b -> p t (j b)", t=TILES)
-                )
-            if far_ahead < GROUPS:
-                transpose_group(far_ahead)
-            if 0 <= ahead < GROUPS:
-                project_group(ahead)
+            if g + 4 < GROUPS:
+                transpose_group(g + 4)
+            if 0 <= g + 3 < GROUPS:
+                copy_group(g + 3)
+            if 0 <= g + 1 < GROUPS:
+                measure_group(g + 1)
+            if g == -3:
+                spread_gain()
+            if 0 <= g + 2 < GROUPS:
+                project_group(g + 2)
+        add_products(GROUPS - 1, None)

@@ -30,17 +30,11 @@ ROUND = 1.5 * 2.0**23
 FLOPS = 2 * BATCH * SEQ * DIM * (LATENT + ROPE)
 
 
-def keep_tensor_busy(nc, identity, out):
-    nc.tensor.matmul(out=out, lhsT=identity[:], rhs=identity[:], start=True, stop=True)
-
-
-def transpose_words(nc, psum_t, identity, rows, busy):
+def transpose_words(nc, psum_t, identity, rows, row_tiles):
     row_words = rows[:].bitcast(F32)
     banks = []
-    for pair, repeats in enumerate(busy):
+    for pair in range(row_tiles // 2):
         flipped = psum_t.tile([P, 2, 2, P], F32)
-        for repeat in range(repeats):
-            keep_tensor_busy(nc, identity, flipped[:, 1, 1, :])
         for t in range(2):
             for u in range(2):
                 row_start = (2 * pair + t) * WORDS
@@ -127,17 +121,17 @@ def tile_simplemla_pa_t_kernel(tc, x, wkv_a, kv_norm_w, out_0, out_1):
         psum_kv = stack.enter_context(tc.psum_pool(name="psum_kv", bufs=2))
         stack.enter_context(tc.manual_schedule())
 
+        gain_row = const.tile([P, LATENT], BF16)
+        nc.vector.memset(gain_row[:], 0.0)
+        ones = const.tile([P, P], BF16)
+        nc.vector.memset(ones[:], 1.0)
+
         w_rows = const.tile([P, 2 * DIM], BF16)
         nc.sync.dma_start(
             out=w_rows[:].rearrange("p (a k) -> p a k", a=2),
             in_=wkv_a.rearrange("(a p) k -> p a k", p=P),
         )
-        gain_row = const.tile([P, LATENT], BF16)
-        nc.vector.memset(gain_row[:], 0.0)
         nc.sync.dma_start(out=gain_row[0:1, :], in_=kv_norm_w.unsqueeze(0))
-        ones = const.tile([P, P], BF16)
-        nc.vector.memset(ones[:], 1.0)
-        gain = const.tile([P, LATENT], F32)
         x_rows = []
         for g in range(GROUPS):
             half, b = divmod(g, BATCH)
@@ -157,7 +151,11 @@ def tile_simplemla_pa_t_kernel(tc, x, wkv_a, kv_norm_w, out_0, out_1):
         tables = [rotation_table(nc, const, phases[0], 0)]
 
         w_grouped = const.tile([P, 2 * DIM], BF16, align_bytes=64)
-        group_words(transpose_words(nc, psum_t, identity, w_rows, [4]), w_grouped, [nc.scalar.copy])
+        group_words(transpose_words(nc, psum_t, identity, w_rows, 2), w_grouped, [nc.scalar.copy])
+        spread = psum_t.tile([P, LATENT], F32, name="flipped")
+        nc.tensor.matmul(out=spread[:], lhsT=ones[:], rhs=gain_row[:], start=True, stop=True)
+        gain = const.tile([P, LATENT], F32)
+        nc.scalar.copy(out=gain[:], in_=spread[:])
         tables.append(rotation_table(nc, const, phases[1], 1))
         preload = const.tile([P, 1], F32)
         nc.scalar.activation(
@@ -174,13 +172,8 @@ def tile_simplemla_pa_t_kernel(tc, x, wkv_a, kv_norm_w, out_0, out_1):
         inv_rms_of = {}
         products_of = {}
 
-        def spread_gain():
-            spread = psum_kv.tile([P, LATENT], F32, name="raw")
-            nc.tensor.matmul(out=spread[:], lhsT=ones[:], rhs=gain_row[:], start=True, stop=True)
-            nc.vector.tensor_copy(out=gain[:], in_=spread[:])
-
         def transpose_group(g):
-            banks_of[g] = transpose_words(nc, psum_t, identity, x_rows[g], (2, 1) if g < 3 else (0, 1))
+            banks_of[g] = transpose_words(nc, psum_t, identity, x_rows[g], TILES)
 
         def copy_group(g):
             x_grouped = work.tile([P, TILES * DIM], BF16, align_bytes=64)
@@ -284,6 +277,8 @@ def tile_simplemla_pa_t_kernel(tc, x, wkv_a, kv_norm_w, out_0, out_1):
             return kv_cache
 
         for g in range(-4, GROUPS):
+            if g == 0:
+                rotate_group(g)
             if 0 <= g + 2 < GROUPS:
                 quantise_group(g + 2)
             if g in (-1, 1):
@@ -291,18 +286,18 @@ def tile_simplemla_pa_t_kernel(tc, x, wkv_a, kv_norm_w, out_0, out_1):
                 nc.vector.tensor_copy(out=table[:, 1, 1], in_=table[:, 0, 0])
             if g >= 1:
                 add_products(g - 1, codes_of[g + 2][0] if g + 2 < GROUPS else None)
-            if g >= 0:
                 rotate_group(g)
+            if g >= 0:
                 kv_cache = normalise_group(g)
                 nc.sync.dma_start(out=output_rows(out_0, g), in_=kv_cache[:])
+            if g < 0 and g + 2 >= 0:
+                project_group(g + 2)
             if g + 4 < GROUPS:
                 transpose_group(g + 4)
             if 0 <= g + 3 < GROUPS:
                 copy_group(g + 3)
             if 0 <= g + 1 < GROUPS:
                 measure_group(g + 1)
-            if g == -3:
-                spread_gain()
-            if 0 <= g + 2 < GROUPS:
+            if 0 <= g and g + 2 < GROUPS:
                 project_group(g + 2)
         add_products(GROUPS - 1, None)

@@ -24,6 +24,8 @@ PER_PARTITION = SEQ // P
 TILES = 4
 HALVES = PER_PARTITION // TILES
 GROUPS = BATCH * HALVES
+ALL_TILES = slice(0, TILES)
+LAST_PIECES = (slice(0, TILES // 2), slice(TILES // 2, TILES))
 
 ROUND = 1.5 * 2.0**23
 
@@ -108,7 +110,17 @@ def rotation_table(nc, const, phases, half):
     nc.scalar.activation(out=table[:, 0, 1], in_=rest[:], func=ACT.Sin, scale=turn)
     nc.scalar.activation(out=table[:, 1, 0], in_=rest[:], func=ACT.Sin, scale=-turn)
     nc.scalar.activation(out=table[:, 0, 0], in_=least[:], func=ACT.Sin, scale=turn, bias=math.pi / 2.0)
+    nc.gpsimd.tensor_scalar(
+        out=table[:, 1, 1], in0=table[:, 0, 0], scalar1=1.0, scalar2=0.0, op0=ALU.mult, op1=ALU.add
+    )
     return table
+
+
+def group_of(tensor, g):
+    half, b = divmod(g, BATCH)
+    return tensor[b].rearrange("(p i) c -> p i c", i=PER_PARTITION)[
+        :, half * TILES : (half + 1) * TILES, :
+    ]
 
 
 def tile_simplemla_pa_t_kernel(tc, x, wkv_a, kv_norm_w, out_0, out_1):
@@ -121,50 +133,43 @@ def tile_simplemla_pa_t_kernel(tc, x, wkv_a, kv_norm_w, out_0, out_1):
         psum_kv = stack.enter_context(tc.psum_pool(name="psum_kv", bufs=2))
         stack.enter_context(tc.manual_schedule())
 
+        turn = rotation_turns(nc, const)
+        identity = const.tile([P, P], F32)
+        make_identity(nc, identity[:])
         gain_row = const.tile([P, LATENT], BF16)
-        nc.vector.memset(gain_row[:], 0.0)
+        nc.gpsimd.memset(gain_row[:], 0.0)
         ones = const.tile([P, P], BF16)
-        nc.vector.memset(ones[:], 1.0)
+        nc.gpsimd.memset(ones[:], 1.0)
 
         w_rows = const.tile([P, 2 * DIM], BF16)
         nc.sync.dma_start(
             out=w_rows[:].rearrange("p (a k) -> p a k", a=2),
             in_=wkv_a.rearrange("(a p) k -> p a k", p=P),
         )
-        nc.sync.dma_start(out=gain_row[0:1, :], in_=kv_norm_w.unsqueeze(0))
         x_rows = []
         for g in range(GROUPS):
-            half, b = divmod(g, BATCH)
             x_group = resident.tile([P, TILES * DIM], BF16)
-            nc.sync.dma_start(
-                out=x_group[:].rearrange("p (i k) -> p i k", i=TILES),
-                in_=x[b].rearrange("(p i) k -> p i k", i=PER_PARTITION)[
-                    :, half * TILES : (half + 1) * TILES, :
-                ],
-            )
+            pieces = 2 if g == 0 else 1
+            for piece in range(pieces):
+                tiles = slice(piece * TILES // pieces, (piece + 1) * TILES // pieces)
+                nc.sync.dma_start(
+                    out=x_group[:].rearrange("p (i k) -> p i k", i=TILES)[:, tiles, :],
+                    in_=group_of(x, g)[:, tiles, :],
+                )
             x_rows.append(x_group)
+            if g == 0:
+                nc.sync.dma_start(out=gain_row[0:1, :], in_=kv_norm_w.unsqueeze(0))
 
-        turn = rotation_turns(nc, const)
-        identity = const.tile([P, P], F32)
-        make_identity(nc, identity[:])
         phases = rotation_phases(nc, const, turn)
-        tables = [rotation_table(nc, const, phases[0], 0)]
-
-        w_grouped = const.tile([P, 2 * DIM], BF16, align_bytes=64)
-        group_words(transpose_words(nc, psum_t, identity, w_rows, 2), w_grouped, [nc.scalar.copy])
-        spread = psum_t.tile([P, LATENT], F32, name="flipped")
-        nc.tensor.matmul(out=spread[:], lhsT=ones[:], rhs=gain_row[:], start=True, stop=True)
-        gain = const.tile([P, LATENT], F32)
-        nc.scalar.copy(out=gain[:], in_=spread[:])
-        tables.append(rotation_table(nc, const, phases[1], 1))
+        tables = [rotation_table(nc, const, phases[half], half) for half in range(HALVES)]
         preload = const.tile([P, 1], F32)
         nc.scalar.activation(
             out=preload[:], in_=identity[:, 0:1], func=ACT.Abs_reciprocal_sqrt, scale=1.0, bias=1.0
         )
+        w_grouped = const.tile([P, 2 * DIM], BF16, align_bytes=64)
         w_codes = const.tile([P, 2 * P], U32, align_bytes=64)
         w_scales = const.tile([P, 2 * P], U8, align_bytes=64)
-        nc.vector.quantize_mx(out=w_codes[:].bitcast(FP8X4), scales=w_scales[:], in_=w_grouped[:])
-
+        gain = const.tile([P, LATENT], F32)
         banks_of = {}
         grouped_of = {}
         codes_of = {}
@@ -176,9 +181,10 @@ def tile_simplemla_pa_t_kernel(tc, x, wkv_a, kv_norm_w, out_0, out_1):
             banks_of[g] = transpose_words(nc, psum_t, identity, x_rows[g], TILES)
 
         def copy_group(g):
-            x_grouped = work.tile([P, TILES * DIM], BF16, align_bytes=64)
-            copies = {0: 2 * [nc.vector.tensor_copy], 1: [nc.vector.tensor_copy, nc.scalar.copy]}
-            group_words(banks_of[g], x_grouped, copies.get(g, 2 * [nc.scalar.copy]))
+            x_grouped = resident.tile([P, TILES * DIM], BF16, align_bytes=64)
+            vector, scalar = nc.vector.tensor_copy, nc.scalar.copy
+            copies = {0: (vector, vector), 1: (vector, scalar)}
+            group_words(banks_of[g], x_grouped, copies.get(g, (scalar, scalar)))
             grouped_of[g] = x_grouped
 
         def quantise_group(g):
@@ -228,76 +234,104 @@ def tile_simplemla_pa_t_kernel(tc, x, wkv_a, kv_norm_w, out_0, out_1):
             )
             inv_rms_of[g] = inv_rms
 
-        def output_rows(out, g):
-            half, b = divmod(g, BATCH)
-            return out[b].rearrange("(p i) c -> p i c", i=PER_PARTITION)[
-                :, half * TILES : (half + 1) * TILES, :
-            ]
-
-        def rotate_group(g):
+        def rotate_tiles(g, tiles):
             half = g // BATCH
-            products = work.tile([P, 2, TILES * PAIRS, 2], F32)
+            columns = (tiles.stop - tiles.start) * PAIRS
+            angles = slice(tiles.start * PAIRS, tiles.stop * PAIRS)
+            products = work.tile([P, 2, columns, 2], F32)
             nc.vector.tensor_tensor(
                 out=products[:],
-                in0=kv_of[g][1][:]
+                in0=kv_of[g][1][:, tiles, :]
                 .rearrange("p t (j a) -> p a (t j)", a=2)
                 .unsqueeze(3)
-                .to_broadcast([P, 2, TILES * PAIRS, 2]),
-                in1=tables[half][:].rearrange("p a b ij -> p a ij b"),
+                .to_broadcast([P, 2, columns, 2]),
+                in1=tables[half][:, :, :, angles].rearrange("p a b ij -> p a ij b"),
                 op=ALU.mult,
             )
-            products_of[g] = products
+            products_of.setdefault(g, []).append((tiles, products))
 
-        def add_products(g, after_codes):
-            if after_codes is not None:
-                waited = work.tile([P, 1], U32)
-                nc.gpsimd.tensor_copy(out=waited[:], in_=after_codes[:, 0:1])
-            products = products_of[g]
-            k_pe = resident.tile([P, TILES * PAIRS, 2], F32)
-            nc.gpsimd.tensor_tensor(
-                out=k_pe[:], in0=products[:, 0], in1=products[:, 1], op=ALU.add
-            )
-            nc.sync.dma_start(
-                out=output_rows(out_1, g), in_=k_pe[:].rearrange("p (t j) b -> p t (j b)", t=TILES)
-            )
+        def rotate_group(g):
+            rotate_tiles(g, ALL_TILES)
 
-        def normalise_group(g):
+        def add_products(g, room):
+            for tiles, products in products_of[g]:
+                columns = slice(tiles.start * ROPE, tiles.stop * ROPE)
+                k_pe = room[:].bitcast(F32)[:, columns]
+                nc.gpsimd.tensor_tensor(
+                    out=k_pe.rearrange("p (ij b) -> p ij b", b=2),
+                    in0=products[:, 0],
+                    in1=products[:, 1],
+                    op=ALU.add,
+                )
+                nc.sync.dma_start(
+                    out=group_of(out_1, g)[:, tiles, :],
+                    in_=k_pe.rearrange("p (t c) -> p t c", c=ROPE),
+                )
+
+        def normalise_tiles(g, tiles):
             latent = kv_of[g][0]
             inv_rms = inv_rms_of[g]
-            kv_cache = resident.tile([P, TILES, LATENT], F32)
-            for t in range(TILES):
+            kv_cache = resident.tile([P, tiles.stop - tiles.start, LATENT], F32)
+            for t in range(tiles.start, tiles.stop):
                 nc.vector.scalar_tensor_tensor(
-                    out=kv_cache[:, t, :],
+                    out=kv_cache[:, t - tiles.start, :],
                     in0=latent[:, t, :],
                     scalar=inv_rms[:, t : t + 1],
                     in1=gain[:],
                     op0=ALU.mult,
                     op1=ALU.mult,
                 )
-            return kv_cache
+            nc.sync.dma_start(out=group_of(out_0, g)[:, tiles, :], in_=kv_cache[:])
 
-        for g in range(-4, GROUPS):
-            if g == 0:
-                rotate_group(g)
-            if 0 <= g + 2 < GROUPS:
+        def normalise_group(g):
+            normalise_tiles(g, ALL_TILES)
+
+        group_words(
+            transpose_words(nc, psum_t, identity, w_rows, 2), w_grouped, (nc.vector.tensor_copy,)
+        )
+        transpose_group(0)
+        copy_group(0)
+        nc.vector.quantize_mx(out=w_codes[:].bitcast(FP8X4), scales=w_scales[:], in_=w_grouped[:])
+        spread = psum_t.tile([P, LATENT], F32, name="flipped")
+        nc.tensor.matmul(out=spread[:], lhsT=ones[:], rhs=gain_row[:], start=True, stop=True)
+        nc.scalar.copy(out=gain[:], in_=spread[:])
+        quantise_group(0)
+        transpose_group(1)
+        copy_group(1)
+        transpose_group(2)
+        project_group(0)
+        quantise_group(1)
+        rotate_group(0)
+        copy_group(2)
+        measure_group(0)
+        transpose_group(3)
+        project_group(1)
+        quantise_group(2)
+        normalise_group(0)
+        copy_group(3)
+        measure_group(1)
+        transpose_group(4)
+        project_group(2)
+
+        last = GROUPS - 1
+        for g in range(1, last):
+            if g + 2 < GROUPS:
                 quantise_group(g + 2)
-            if g in (-1, 1):
-                table = tables[0 if g == -1 else 1]
-                nc.vector.tensor_copy(out=table[:, 1, 1], in_=table[:, 0, 0])
-            if g >= 1:
-                add_products(g - 1, codes_of[g + 2][0] if g + 2 < GROUPS else None)
-                rotate_group(g)
-            if g >= 0:
-                kv_cache = normalise_group(g)
-                nc.sync.dma_start(out=output_rows(out_0, g), in_=kv_cache[:])
-            if g < 0 and g + 2 >= 0:
-                project_group(g + 2)
+            add_products(g - 1, grouped_of[g + 2] if g + 2 < GROUPS else grouped_of[0])
+            rotate_group(g)
+            normalise_group(g)
             if g + 4 < GROUPS:
                 transpose_group(g + 4)
-            if 0 <= g + 3 < GROUPS:
+            if g + 3 < GROUPS:
                 copy_group(g + 3)
-            if 0 <= g + 1 < GROUPS:
+            if g + 1 < GROUPS:
                 measure_group(g + 1)
-            if 0 <= g and g + 2 < GROUPS:
+            if g + 2 < GROUPS:
                 project_group(g + 2)
-        add_products(GROUPS - 1, None)
+
+        add_products(last - 1, grouped_of[1])
+        for tiles in LAST_PIECES:
+            rotate_tiles(last, tiles)
+        add_products(last, grouped_of[2])
+        for tiles in LAST_PIECES:
+            normalise_tiles(last, tiles)

@@ -199,9 +199,9 @@ def tile_simplemla_pa_t_kernel(tc, x, wkv_a, kv_norm_w, out_0, out_1):
             x_codes, x_scales = codes_of[g]
             latent = psum_kv.tile([P, TILES, LATENT], F32)
             raw = psum_kv.tile([P, TILES, ROPE], F32)
-            for t in range(TILES):
-                tokens = slice(t * P, (t + 1) * P)
-                for result, columns in ((latent, slice(0, LATENT)), (raw, slice(LATENT, LATENT + ROPE))):
+            for result, columns in ((latent, slice(0, LATENT)), (raw, slice(LATENT, LATENT + ROPE))):
+                for t in range(TILES):
+                    tokens = slice(t * P, (t + 1) * P)
                     nc.tensor.matmul_mx(
                         out=result[:, t, :],
                         lhsT=x_codes[:, tokens].bitcast(FP8X4),
@@ -318,8 +318,8 @@ def tile_simplemla_pa_t_kernel(tc, x, wkv_a, kv_norm_w, out_0, out_1):
             if g + 2 < GROUPS:
                 quantise_group(g + 2)
             add_products(g - 1, grouped_of[g + 2] if g + 2 < GROUPS else grouped_of[0])
-            rotate_group(g)
             normalise_group(g)
+            rotate_group(g)
             if g + 4 < GROUPS:
                 transpose_group(g + 4)
             if g + 3 < GROUPS:
@@ -331,7 +331,7 @@ def tile_simplemla_pa_t_kernel(tc, x, wkv_a, kv_norm_w, out_0, out_1):
 
         add_products(last - 1, grouped_of[1])
         for tiles in LAST_PIECES:
+            normalise_tiles(last, tiles)
+        for tiles in LAST_PIECES:
             rotate_tiles(last, tiles)
         add_products(last, grouped_of[2])
-        for tiles in LAST_PIECES:
-            normalise_tiles(last, tiles)

@@ -24,8 +24,8 @@ PER_PARTITION = SEQ // P
 TILES = 4
 HALVES = PER_PARTITION // TILES
 GROUPS = BATCH * HALVES
-ALL_TILES = slice(0, TILES)
-LAST_PIECES = (slice(0, TILES // 2), slice(TILES // 2, TILES))
+WHOLE = (slice(0, TILES),)
+PIECES = (slice(0, TILES // 2), slice(TILES // 2, TILES))
 
 ROUND = 1.5 * 2.0**23
 
@@ -234,57 +234,54 @@ def tile_simplemla_pa_t_kernel(tc, x, wkv_a, kv_norm_w, out_0, out_1):
             )
             inv_rms_of[g] = inv_rms
 
-        def rotate_tiles(g, tiles):
+        def rotate_group(g, pieces):
             half = g // BATCH
-            columns = (tiles.stop - tiles.start) * PAIRS
-            angles = slice(tiles.start * PAIRS, tiles.stop * PAIRS)
-            products = work.tile([P, 2, columns, 2], F32)
-            nc.vector.tensor_tensor(
-                out=products[:],
-                in0=kv_of[g][1][:, tiles, :]
-                .rearrange("p t (j a) -> p a (t j)", a=2)
-                .unsqueeze(3)
-                .to_broadcast([P, 2, columns, 2]),
-                in1=tables[half][:, :, :, angles].rearrange("p a b ij -> p a ij b"),
-                op=ALU.mult,
-            )
-            products_of.setdefault(g, []).append((tiles, products))
+            products = resident.tile([P, 2, TILES * PAIRS, 2], F32)
+            for tiles in pieces:
+                columns = (tiles.stop - tiles.start) * PAIRS
+                angles = slice(tiles.start * PAIRS, tiles.stop * PAIRS)
+                nc.vector.tensor_tensor(
+                    out=products[:, :, angles, :],
+                    in0=kv_of[g][1][:, tiles, :]
+                    .rearrange("p t (j a) -> p a (t j)", a=2)
+                    .unsqueeze(3)
+                    .to_broadcast([P, 2, columns, 2]),
+                    in1=tables[half][:, :, :, angles].rearrange("p a b ij -> p a ij b"),
+                    op=ALU.mult,
+                )
+            products_of[g] = products
 
-        def rotate_group(g):
-            rotate_tiles(g, ALL_TILES)
+        def room_of(g, half):
+            columns = slice(half * TILES * ROPE, (half + 1) * TILES * ROPE)
+            return grouped_of[g][:].bitcast(F32)[:, columns].rearrange("p (t c) -> p t c", t=TILES)
 
-        def add_products(g, room):
-            for tiles, products in products_of[g]:
-                columns = slice(tiles.start * ROPE, tiles.stop * ROPE)
-                k_pe = room[:].bitcast(F32)[:, columns]
-                nc.gpsimd.tensor_tensor(
-                    out=k_pe.rearrange("p (ij b) -> p ij b", b=2),
-                    in0=products[:, 0],
-                    in1=products[:, 1],
+        def add_products(g, pieces, room, engine=nc.gpsimd):
+            k_pe = room_of(room, 0)
+            for tiles in pieces:
+                angles = slice(tiles.start * PAIRS, tiles.stop * PAIRS)
+                engine.tensor_tensor(
+                    out=k_pe[:, tiles, :].rearrange("p t (j b) -> p (t j) b", b=2),
+                    in0=products_of[g][:, 0, angles, :],
+                    in1=products_of[g][:, 1, angles, :],
                     op=ALU.add,
                 )
-                nc.sync.dma_start(
-                    out=group_of(out_1, g)[:, tiles, :],
-                    in_=k_pe.rearrange("p (t c) -> p t c", c=ROPE),
-                )
+                nc.sync.dma_start(out=group_of(out_1, g)[:, tiles, :], in_=k_pe[:, tiles, :])
 
-        def normalise_tiles(g, tiles):
+        def normalise_group(g, pieces):
             latent = kv_of[g][0]
             inv_rms = inv_rms_of[g]
-            kv_cache = resident.tile([P, tiles.stop - tiles.start, LATENT], F32)
-            for t in range(tiles.start, tiles.stop):
-                nc.vector.scalar_tensor_tensor(
-                    out=kv_cache[:, t - tiles.start, :],
-                    in0=latent[:, t, :],
-                    scalar=inv_rms[:, t : t + 1],
-                    in1=gain[:],
-                    op0=ALU.mult,
-                    op1=ALU.mult,
-                )
-            nc.sync.dma_start(out=group_of(out_0, g)[:, tiles, :], in_=kv_cache[:])
-
-        def normalise_group(g):
-            normalise_tiles(g, ALL_TILES)
+            kv_cache = room_of(g, 1)
+            for tiles in pieces:
+                for t in range(tiles.start, tiles.stop):
+                    nc.vector.scalar_tensor_tensor(
+                        out=kv_cache[:, t, :],
+                        in0=latent[:, t, :],
+                        scalar=inv_rms[:, t : t + 1],
+                        in1=gain[:],
+                        op0=ALU.mult,
+                        op1=ALU.mult,
+                    )
+                nc.sync.dma_start(out=group_of(out_0, g)[:, tiles, :], in_=kv_cache[:, tiles, :])
 
         group_words(
             transpose_words(nc, psum_t, identity, w_rows, 2), w_grouped, (nc.vector.tensor_copy,)
@@ -292,22 +289,22 @@ def tile_simplemla_pa_t_kernel(tc, x, wkv_a, kv_norm_w, out_0, out_1):
         transpose_group(0)
         copy_group(0)
         nc.vector.quantize_mx(out=w_codes[:].bitcast(FP8X4), scales=w_scales[:], in_=w_grouped[:])
-        spread = psum_t.tile([P, LATENT], F32, name="flipped")
-        nc.tensor.matmul(out=spread[:], lhsT=ones[:], rhs=gain_row[:], start=True, stop=True)
-        nc.scalar.copy(out=gain[:], in_=spread[:])
         quantise_group(0)
         transpose_group(1)
         copy_group(1)
         transpose_group(2)
         project_group(0)
+        spread = psum_t.tile([P, LATENT], F32, name="flipped")
+        nc.tensor.matmul(out=spread[:], lhsT=ones[:], rhs=gain_row[:], start=True, stop=True)
         quantise_group(1)
-        rotate_group(0)
+        rotate_group(0, WHOLE)
         copy_group(2)
+        nc.scalar.copy(out=gain[:], in_=spread[:])
         measure_group(0)
         transpose_group(3)
         project_group(1)
         quantise_group(2)
-        normalise_group(0)
+        normalise_group(0, WHOLE)
         copy_group(3)
         measure_group(1)
         transpose_group(4)
@@ -317,9 +314,9 @@ def tile_simplemla_pa_t_kernel(tc, x, wkv_a, kv_norm_w, out_0, out_1):
         for g in range(1, last):
             if g + 2 < GROUPS:
                 quantise_group(g + 2)
-            add_products(g - 1, grouped_of[g + 2] if g + 2 < GROUPS else grouped_of[0])
-            normalise_group(g)
-            rotate_group(g)
+            add_products(g - 1, WHOLE, g + 2 if g + 2 < GROUPS else 0)
+            normalise_group(g, WHOLE)
+            rotate_group(g, WHOLE)
             if g + 4 < GROUPS:
                 transpose_group(g + 4)
             if g + 3 < GROUPS:
@@ -329,9 +326,8 @@ def tile_simplemla_pa_t_kernel(tc, x, wkv_a, kv_norm_w, out_0, out_1):
             if g + 2 < GROUPS:
                 project_group(g + 2)
 
-        add_products(last - 1, grouped_of[1])
-        for tiles in LAST_PIECES:
-            normalise_tiles(last, tiles)
-        for tiles in LAST_PIECES:
-            rotate_tiles(last, tiles)
-        add_products(last, grouped_of[2])
+        add_products(last - 1, WHOLE, 1)
+        rotate_group(last, PIECES)
+        normalise_group(last, PIECES)
+        add_products(last, PIECES[:1], 2)
+        add_products(last, PIECES[1:], 2, nc.vector)

import math
from contextlib import ExitStack

import concourse.mybir as mybir
from concourse.masks import make_identity

F32 = mybir.dt.float32
BF16 = mybir.dt.bfloat16
U32 = mybir.dt.uint32
U8 = mybir.dt.uint8
FP8X4 = mybir.dt.float8_e4m3fn_x4
ALU = mybir.AluOpType
ACT = mybir.ActivationFunctionType

P = 128
BATCH, SEQ, DIM = 8, 1024, 512
LATENT, ROPE = 128, 128
PAIRS = ROPE // 2
THETA = 10000.0
EPS = 1e-6

WORDS = DIM // 2
PER_PARTITION = SEQ // P
TILES = 4
HALVES = PER_PARTITION // TILES
GROUPS = BATCH * HALVES
WHOLE = (slice(0, TILES),)
PIECES = (slice(0, TILES // 2), slice(TILES // 2, TILES))

ROUND = 1.5 * 2.0**23

FLOPS = 2 * BATCH * SEQ * DIM * (LATENT + ROPE)


def transpose_words(nc, psum_t, identity, rows, row_tiles):
    row_words = rows[:].bitcast(F32)
    banks = []
    for pair in range(row_tiles // 2):
        flipped = psum_t.tile([P, 2, 2, P], F32)
        for t in range(2):
            for u in range(2):
                row_start = (2 * pair + t) * WORDS
                nc.tensor.transpose(
                    flipped[:, t, u, :], row_words[:, row_start + u : row_start + WORDS : 2], identity[:]
                )
        banks.append(flipped)
    return banks


def group_words(banks, grouped, copies):
    grouped_words = grouped[:].bitcast(F32)
    for pair, (flipped, copy) in enumerate(zip(banks, copies)):
        copy(
            out=grouped_words[:, 2 * pair * WORDS : 2 * (pair + 1) * WORDS].rearrange(
                "p (t r u) -> p t r u", t=2, u=2
            ),
            in_=flipped[:].rearrange("p t u r -> p t r u"),
        )


def rotation_turns(nc, const):
    position = const.tile([P, PER_PARTITION], F32)
    nc.gpsimd.iota(
        position[:],
        pattern=[[1, PER_PARTITION]],
        base=0,
        channel_multiplier=PER_PARTITION,
        allow_small_or_imprecise_dtypes=True,
    )
    turn = const.tile([P, PER_PARTITION, PAIRS], F32)
    nc.vector.tensor_scalar_mul(
        out=turn[:, :, 0:1], in0=position[:].unsqueeze(2), scalar1=1.0 / (2.0 * math.pi)
    )
    done = 1
    while done < PAIRS:
        for copy in range(1, 4):
            nc.vector.tensor_scalar_mul(
                out=turn[:, :, copy * done : (copy + 1) * done],
                in0=turn[:, :, 0:done],
                scalar1=THETA ** (-2.0 * copy * done / ROPE),
            )
        done *= 4
    return turn[:].rearrange("p (h i) j -> p h (i j)", h=HALVES)


def rotation_phases(nc, const, turn):
    whole, rest, least = (
        [const.tile([P, TILES * PAIRS], F32, name=f"{what}_{half}") for half in range(HALVES)]
        for what in ("whole", "rest", "least")
    )
    for half in range(HALVES):
        nc.vector.tensor_scalar(
            out=whole[half][:], in0=turn[:, half], scalar1=ROUND, scalar2=ROUND, op0=ALU.add, op1=ALU.subtract
        )
    for half in range(HALVES):
        nc.vector.tensor_tensor(
            out=rest[half][:], in0=turn[:, half], in1=whole[half][:], op=ALU.subtract
        )
    for half in range(HALVES):
        nc.vector.scalar_tensor_tensor(
            out=least[half][:], in0=rest[half][:], scalar=-1.0, in1=rest[half][:], op0=ALU.mult, op1=ALU.min
        )
    return list(zip(rest, least))


def rotation_table(nc, const, phases, half):
    rest, least = phases
    turn = 2.0 * math.pi
    table = const.tile([P, 2, 2, TILES * PAIRS], F32, name=f"table_{half}")
    nc.scalar.activation(out=table[:, 0, 1], in_=rest[:], func=ACT.Sin, scale=turn)
    nc.scalar.activation(out=table[:, 1, 0], in_=rest[:], func=ACT.Sin, scale=-turn)
    nc.scalar.activation(out=table[:, 0, 0], in_=least[:], func=ACT.Sin, scale=turn, bias=math.pi / 2.0)
    nc.gpsimd.tensor_scalar(
        out=table[:, 1, 1], in0=table[:, 0, 0], scalar1=1.0, scalar2=0.0, op0=ALU.mult, op1=ALU.add
    )
    return table


def group_of(tensor, g):
    half, b = divmod(g, BATCH)
    return tensor[b].rearrange("(p i) c -> p i c", i=PER_PARTITION)[
        :, half * TILES : (half + 1) * TILES, :
    ]


def tile_simplemla_pa_t_kernel(tc, x, wkv_a, kv_norm_w, out_0, out_1):
    nc = tc.nc
    with ExitStack() as stack:
        const = stack.enter_context(tc.tile_pool(name="const", bufs=1))
        resident = stack.enter_context(tc.tile_pool(name="resident", bufs=GROUPS))
        work = stack.enter_context(tc.tile_pool(name="work", bufs=3))
        psum_t = stack.enter_context(tc.psum_pool(name="psum_t", bufs=4))
        psum_kv = stack.enter_context(tc.psum_pool(name="psum_kv", bufs=2))
        stack.enter_context(tc.manual_schedule())

        turn = rotation_turns(nc, const)
        identity = const.tile([P, P], F32)
        make_identity(nc, identity[:])
        gain_row = const.tile([P, LATENT], BF16)
        nc.gpsimd.memset(gain_row[:], 0.0)
        ones = const.tile([P, P], BF16)
        nc.gpsimd.memset(ones[:], 1.0)

        w_rows = const.tile([P, 2 * DIM], BF16)
        nc.sync.dma_start(
            out=w_rows[:].rearrange("p (a k) -> p a k", a=2),
            in_=wkv_a.rearrange("(a p) k -> p a k", p=P),
        )
        x_rows = []
        for g in range(GROUPS):
            x_group = resident.tile([P, TILES * DIM], BF16)
            pieces = 2 if g == 0 else 1
            for piece in range(pieces):
                tiles = slice(piece * TILES // pieces, (piece + 1) * TILES // pieces)
                nc.sync.dma_start(
                    out=x_group[:].rearrange("p (i k) -> p i k", i=TILES)[:, tiles, :],
                    in_=group_of(x, g)[:, tiles, :],
                )
            x_rows.append(x_group)
            if g == 0:
                nc.sync.dma_start(out=gain_row[0:1, :], in_=kv_norm_w.unsqueeze(0))

        phases = rotation_phases(nc, const, turn)
        tables = [rotation_table(nc, const, phases[half], half) for half in range(HALVES)]
        preload = const.tile([P, 1], F32)
        nc.scalar.activation(
            out=preload[:], in_=identity[:, 0:1], func=ACT.Abs_reciprocal_sqrt, scale=1.0, bias=1.0
        )
        w_grouped = const.tile([P, 2 * DIM], BF16, align_bytes=64)
        w_codes = const.tile([P, 2 * P], U32, align_bytes=64)
        w_scales = const.tile([P, 2 * P], U8, align_bytes=64)
        gain = const.tile([P, LATENT], F32)
        banks_of = {}
        grouped_of = {}
        codes_of = {}
        kv_of = {}
        inv_rms_of = {}
        products_of = {}

        def transpose_group(g):
            banks_of[g] = transpose_words(nc, psum_t, identity, x_rows[g], TILES)

        def copy_group(g):
            x_grouped = resident.tile([P, TILES * DIM], BF16, align_bytes=64)
            vector, scalar = nc.vector.tensor_copy, nc.scalar.copy
            copies = {0: (vector, vector), 1: (vector, scalar)}
            group_words(banks_of[g], x_grouped, copies.get(g, (scalar, scalar)))
            grouped_of[g] = x_grouped

        def quantise_group(g):
            x_codes = work.tile([P, TILES * P], U32, align_bytes=64)
            x_scales = work.tile([P, TILES * P], U8, align_bytes=64)
            nc.vector.quantize_mx(
                out=x_codes[:].bitcast(FP8X4), scales=x_scales[:], in_=grouped_of[g][:]
            )
            codes_of[g] = (x_codes, x_scales)

        def project_group(g):
            x_codes, x_scales = codes_of[g]
            latent = psum_kv.tile([P, TILES, LATENT], F32)
            raw = psum_kv.tile([P, TILES, ROPE], F32)
            for result, columns in ((latent, slice(0, LATENT)), (raw, slice(LATENT, LATENT + ROPE))):
                for t in range(TILES):
                    tokens = slice(t * P, (t + 1) * P)
                    nc.tensor.matmul_mx(
                        out=result[:, t, :],
                        lhsT=x_codes[:, tokens].bitcast(FP8X4),
                        lhsT_scale=x_scales[:, tokens],
                        rhs=w_codes[:, columns].bitcast(FP8X4),
                        rhs_scale=w_scales[:, columns],
                        start=True,
                        stop=True,
                    )
            kv_of[g] = (latent, raw)

        def measure_group(g):
            latent = kv_of[g][0]
            squares = work.tile([P, TILES, LATENT], F32)
            sum_squares = work.tile([P, TILES], F32)
            for t in range(TILES):
                nc.scalar.activation(
                    out=squares[:, t, :],
                    in_=latent[:, t, :],
                    func=ACT.Square,
                    accum_out=sum_squares[:, t : t + 1],
                )
            inv_rms = work.tile([P, TILES], F32)
            nc.scalar.activation(
                out=inv_rms[:],
                in_=sum_squares[:],
                func=ACT.Abs_reciprocal_sqrt,
                scale=1.0 / LATENT,
                bias=EPS,
            )
            inv_rms_of[g] = inv_rms

        def rotate_group(g, pieces):
            half = g // BATCH
            products = resident.tile([P, 2, TILES * PAIRS, 2], F32)
            for tiles in pieces:
                columns = (tiles.stop - tiles.start) * PAIRS
                angles = slice(tiles.start * PAIRS, tiles.stop * PAIRS)
                nc.vector.tensor_tensor(
                    out=products[:, :, angles, :],
                    in0=kv_of[g][1][:, tiles, :]
                    .rearrange("p t (j a) -> p a (t j)", a=2)
                    .unsqueeze(3)
                    .to_broadcast([P, 2, columns, 2]),
                    in1=tables[half][:, :, :, angles].rearrange("p a b ij -> p a ij b"),
                    op=ALU.mult,
                )
            products_of[g] = products

        def room_of(g, half):
            columns = slice(half * TILES * ROPE, (half + 1) * TILES * ROPE)
            return grouped_of[g][:].bitcast(F32)[:, columns].rearrange("p (t c) -> p t c", t=TILES)

        def add_products(g, pieces, room, engine=nc.gpsimd):
            k_pe = room_of(room, 0)
            for tiles in pieces:
                angles = slice(tiles.start * PAIRS, tiles.stop * PAIRS)
                engine.tensor_tensor(
                    out=k_pe[:, tiles, :].rearrange("p t (j b) -> p (t j) b", b=2),
                    in0=products_of[g][:, 0, angles, :],
                    in1=products_of[g][:, 1, angles, :],
                    op=ALU.add,
                )
                nc.sync.dma_start(out=group_of(out_1, g)[:, tiles, :], in_=k_pe[:, tiles, :])

        def normalise_group(g, pieces):
            latent = kv_of[g][0]
            inv_rms = inv_rms_of[g]
            kv_cache = room_of(g, 1)
            for tiles in pieces:
                for t in range(tiles.start, tiles.stop):
                    nc.vector.scalar_tensor_tensor(
                        out=kv_cache[:, t, :],
                        in0=latent[:, t, :],
                        scalar=inv_rms[:, t : t + 1],
                        in1=gain[:],
                        op0=ALU.mult,
                        op1=ALU.mult,
                    )
                nc.sync.dma_start(out=group_of(out_0, g)[:, tiles, :], in_=kv_cache[:, tiles, :])

        group_words(
            transpose_words(nc, psum_t, identity, w_rows, 2), w_grouped, (nc.vector.tensor_copy,)
        )
        transpose_group(0)
        copy_group(0)
        nc.vector.quantize_mx(out=w_codes[:].bitcast(FP8X4), scales=w_scales[:], in_=w_grouped[:])
        quantise_group(0)
        transpose_group(1)
        copy_group(1)
        transpose_group(2)
        project_group(0)
        spread = psum_t.tile([P, LATENT], F32, name="flipped")
        nc.tensor.matmul(out=spread[:], lhsT=ones[:], rhs=gain_row[:], start=True, stop=True)
        quantise_group(1)
        rotate_group(0, WHOLE)
        copy_group(2)
        nc.scalar.copy(out=gain[:], in_=spread[:])
        measure_group(0)
        transpose_group(3)
        project_group(1)
        quantise_group(2)
        normalise_group(0, WHOLE)
        copy_group(3)
        measure_group(1)
        transpose_group(4)
        project_group(2)

        last = GROUPS - 1
        for g in range(1, last):
            if g + 2 < GROUPS:
                quantise_group(g + 2)
            add_products(g - 1, WHOLE, g + 2 if g + 2 < GROUPS else 0)
            normalise_group(g, WHOLE)
            rotate_group(g, WHOLE)
            if g + 4 < GROUPS:
                transpose_group(g + 4)
            if g + 3 < GROUPS:
                copy_group(g + 3)
            if g + 1 < GROUPS:
                measure_group(g + 1)
            if g + 2 < GROUPS:
                project_group(g + 2)

        add_products(last - 1, WHOLE, 1)
        rotate_group(last, PIECES)
        normalise_group(last, PIECES)
        add_products(last, PIECES[:1], 2)
        add_products(last, PIECES[1:], 2, nc.vector)
